import numpy as np
import ml_dtypes


def mxq(x, axis, fmt="e4m3"):
    dtype, down = {"e4m3": (ml_dtypes.float8_e4m3fn, 7), "e5m2": (ml_dtypes.float8_e5m2, 14)}[fmt]
    v = np.moveaxis(np.asarray(x, np.float32).astype(ml_dtypes.bfloat16).astype(np.float64), axis, -1)
    blocks = v.reshape(v.shape[:-1] + (-1, 32))
    amax = np.abs(blocks).max(-1, keepdims=True)
    byte = np.maximum(np.where(amax > 0, np.frexp(amax)[1] - 1 + 127, 0) - down, 1)
    scale = np.exp2(byte - 127.0)
    codes = (blocks / scale).astype(np.float32).astype(dtype).astype(np.float64)
    return np.moveaxis((codes * scale).reshape(v.shape), -1, axis)


WIDE = False


def mx_kscale(k):
    if not WIDE:
        return np.ones(k)
    levels = np.array([10, -10, 5, -5, 0])
    a = np.random.permutation(np.resize(levels, k // 512 * 4)).reshape(k // 512, 4)
    idx = np.arange(k)
    return np.exp2(a[idx // 512, idx % 128 // 32])


BF16 = ml_dtypes.bfloat16


def bf(x):
    return np.asarray(x, np.float32).astype(BF16)


def f64(x):
    return np.asarray(x).astype(np.float64)


E2M1 = np.array([0.0, 0.5, 1.0, 1.5, 2.0, 3.0, 4.0, 6.0, -0.0, -0.5, -1.0, -1.5, -2.0, -3.0, -4.0, -6.0])


def pack_weight(w, fmt):
    k, n = w.shape
    w = f64(bf(w)).reshape(k // 32, 32, n)
    amax = np.abs(w).max(1)
    if fmt == "e4m3":
        byte = np.frexp(amax)[1] - 1 + 127 - 7
    else:
        mant, ex = np.frexp(amax / 6.0)
        byte = np.where(mant > 0.5, ex, ex - 1) + 127
    byte = np.clip(np.where(amax > 0, byte, 1), 1, 254)
    scaled = (w * np.exp2(127.0 - byte)[:, None, :]).reshape(k, n).astype(np.float32)
    by_word = np.ascontiguousarray(scaled.reshape(k // 512, 128, 4, n).transpose(0, 1, 3, 2))
    if fmt == "e4m3":
        words = by_word.astype(ml_dtypes.float8_e4m3fn).view(np.uint8)
    else:
        c = by_word.astype(ml_dtypes.float4_e2m1fn).view(np.uint8) & 0xF
        words = c[..., 0::2] | (c[..., 1::2] << 4)
    return np.ascontiguousarray(words), np.ascontiguousarray(byte.astype(np.uint8).reshape(k // 512, 16, n))


def unpack_weight(words, scales, fmt):
    g, p, n, _ = words.shape
    if fmt == "e4m3":
        vals = np.ascontiguousarray(words).view(ml_dtypes.float8_e4m3fn).astype(np.float64)
    else:
        nib = np.empty((g, p, n, 4), np.uint8)
        nib[..., 0::2] = words & 0xF
        nib[..., 1::2] = words >> 4
        vals = E2M1[nib]
    vals = vals * np.repeat(np.exp2(scales.astype(np.float64) - 127.0), 8, axis=1)[..., None]
    return vals.transpose(0, 1, 3, 2).reshape(g * 512, n)


B, P0, P1, P2, K0, K1, K2 = 128, 4096, 9216, 7168, 512, 512, 512
PT = P0 + P1 + P2
KT = K0 + K1 + K2
CLIP1 = 1.0
FMT = "e4m3"


def clip_rows(mat, clip):
    norms = np.sqrt(np.sum(mat * mat, axis=1, keepdims=True))
    scale = np.minimum(clip / norms, 1.0)
    return mat * scale


def setup_inputs():
    t0, t1, t2 = mx_kscale(K0), mx_kscale(K1), mx_kscale(K2)
    r = np.exp2(np.random.uniform(-2.0, 2.0, (B, 1))) / (KT * PT) ** 0.25
    target_grad = bf(np.random.standard_normal((B, PT)) * r)
    embedding = bf(np.random.standard_normal((B, KT)) * r * np.concatenate([t0, t1, t2]))
    words0, scales0 = pack_weight(np.ascontiguousarray((np.random.standard_normal((P0, K0)) / np.sqrt(P0) / t0[None, :]).T), FMT)
    words1, scales1 = pack_weight(np.ascontiguousarray((np.random.standard_normal((P1, K1)) / np.sqrt(P1) / t1[None, :]).T), FMT)
    words2, scales2 = pack_weight(np.ascontiguousarray((np.random.standard_normal((P2, K2)) / np.sqrt(P2) / t2[None, :]).T), FMT)
    return {"target_grad": target_grad,
            "embedding": embedding,
            "bases0_words": words0, "bases0_scales": scales0,
            "bases1_words": words1, "bases1_scales": scales1,
            "bases2_words": words2, "bases2_scales": scales2}


def reference(target_grad, embedding, bases0_words, bases0_scales, bases1_words, bases1_scales, bases2_words, bases2_scales):
    g = f64(target_grad)
    e = f64(embedding)
    approx_parts = []
    offset = 0
    for bt in (unpack_weight(bases0_words, bases0_scales, FMT),
               unpack_weight(bases1_words, bases1_scales, FMT),
               unpack_weight(bases2_words, bases2_scales, FMT)):
        num_k = bt.shape[0]
        approx_parts.append(mxq(e[:, offset:offset + num_k], 1, "e4m3") @ bt)
        offset += num_k
    no_reduction_approx = np.concatenate(approx_parts, axis=1)
    residual = g - no_reduction_approx
    return np.sum(clip_rows(residual, CLIP1), axis=0) / B

@@ -1,0 +1,206 @@
+from contextlib import ExitStack
+
+import concourse.mybir as mybir
+from concourse.masks import make_identity
+
+F32 = mybir.dt.float32
+BF16 = mybir.dt.bfloat16
+I32 = mybir.dt.int32
+U32 = mybir.dt.uint32
+U8 = mybir.dt.uint8
+FP8X4 = mybir.dt.float8_e4m3fn_x4
+ALU = mybir.AluOpType
+ACT = mybir.ActivationFunctionType
+AXIS = mybir.AxisListType
+
+P = 128
+K_GROUP = 512
+WIDTHS = (4096, 9216, 7168)
+COLS = sum(WIDTHS)
+BANK = 512
+PASS = 256
+PLANES = 4
+PIECE = 3072
+BLOCKS = COLS // P
+BANKS = COLS // BANK
+GPSIMD_BANKS = 26
+
+FLOPS = 2 * P * K_GROUP * COLS
+
+
+def tile_gep_pb_kernel(
+    tc,
+    target_grad,
+    embedding,
+    bases0_words,
+    bases0_scales,
+    bases1_words,
+    bases1_scales,
+    bases2_words,
+    bases2_scales,
+    out,
+):
+    nc = tc.nc
+    words_in = (bases0_words, bases1_words, bases2_words)
+    scales_in = (bases0_scales, bases1_scales, bases2_scales)
+    groups = len(WIDTHS)
+
+    with ExitStack() as ctx:
+        keep = ctx.enter_context(tc.tile_pool(name="keep", bufs=1))
+        words_pool = ctx.enter_context(tc.tile_pool(name="words", bufs=4))
+        grad_pool = ctx.enter_context(tc.tile_pool(name="grad", bufs=4))
+        square_pool = ctx.enter_context(tc.tile_pool(name="square", bufs=3))
+        acc_pool = ctx.enter_context(tc.psum_pool(name="acc", bufs=4))
+        flip_pool = ctx.enter_context(tc.psum_pool(name="flip", bufs=2))
+        mean_pool = ctx.enter_context(tc.psum_pool(name="mean", bufs=1))
+
+        plane_cols = [width // PLANES for width in WIDTHS]
+        plane_start = [sum(plane_cols[:i]) for i in range(groups)]
+        planes = keep.tile([P, sum(plane_cols)], U8, align_bytes=64)
+        nc.vector.memset(planes[:].bitcast(I32), 0)
+
+        mean_sb = keep.tile([P, 2 * P], F32)
+        nc.vector.memset(mean_sb[:], 0.0)
+
+        ident = keep.tile([P, P], F32)
+        make_identity(nc, ident[:])
+
+        one = keep.tile([P, 1], F32)
+        nc.vector.memset(one[:], 1.0)
+        warm = keep.tile([P, 1], F32)
+        nc.scalar.sqrt(out=warm[:], in_=one[:])
+
+        emb = keep.tile([P, groups * K_GROUP], BF16)
+        nc.sync.dma_start(out=emb[:], in_=embedding)
+        for i in range(groups):
+            cols = slice(plane_start[i], plane_start[i] + plane_cols[i])
+            for quad in range(4):
+                rows = scales_in[i][0, 4 * quad : 4 * quad + 4, :].bitcast(I32)
+                nc.sync.dma_start(
+                    out=planes[32 * quad : 32 * quad + 4 * PLANES, cols].bitcast(I32),
+                    in_=rows.rearrange("r (k c) -> k r c", k=PLANES),
+                )
+
+        emb_words = emb[:].bitcast(F32)
+        grouped = keep.tile([P, groups, 4 * P], BF16, align_bytes=64)
+        emb_codes = keep.tile([P, groups, P], U32, align_bytes=64)
+        emb_scales = keep.tile([P, groups, P], U8, align_bytes=64)
+        for i in range(groups):
+            flipped = flip_pool.tile([P, 2, P], F32, tag="flip")
+            for u in range(2):
+                nc.tensor.transpose(
+                    flipped[:, u, :],
+                    emb_words[:, 256 * i + u : 256 * (i + 1) : 2],
+                    ident[:],
+                )
+            nc.vector.tensor_copy(
+                out=grouped[:, i, :].bitcast(F32).rearrange("p (b u) -> p b u", u=2),
+                in_=flipped[:].rearrange("p u b -> p b u"),
+            )
+        for i in range(groups):
+            nc.vector.quantize_mx(
+                out=emb_codes[:, i, :].bitcast(FP8X4),
+                scales=emb_scales[:, i, :],
+                in_=grouped[:, i, :],
+            )
+
+        residual = keep.tile([P, COLS], F32)
+        square_sums = keep.tile([P, BANKS], F32)
+        halves = residual[:].bitcast(BF16)
+        low = keep.tile([P, COLS], BF16)
+
+        def high(first, count):
+            return halves[:, 2 * first + 1 : 2 * (first + count) : 2]
+
+        def take_low(engine, j):
+            engine.tensor_tensor(
+                out=low[:, j : j + BANK],
+                in0=residual[:, j : j + BANK],
+                in1=high(j, BANK),
+                op=ALU.subtract,
+            )
+
+        first_col = 0
+        for i in range(groups):
+            base_words = words_in[i].rearrange("o p n t -> (o p) (n t)").bitcast(I32)
+            for start in range(0, WIDTHS[i], PIECE):
+                width = min(PIECE, WIDTHS[i] - start)
+                words = words_pool.tile([P, PIECE], U32, align_bytes=64)
+                nc.sync.dma_start(
+                    out=words[:, :width].bitcast(I32), in_=base_words[:, start : start + width]
+                )
+                grad = grad_pool.tile([P, PIECE], BF16)
+                nc.sync.dma_start(
+                    out=grad[:, :width],
+                    in_=target_grad[:, first_col + start : first_col + start + width],
+                )
+                for c in range(0, width, BANK):
+                    acc = acc_pool.tile([P, BANK], F32)
+                    for h in range(0, BANK, PASS):
+                        n = start + c + h
+                        k = n // plane_cols[i]
+                        s = plane_start[i] + n % plane_cols[i]
+                        nc.tensor.matmul_mx(
+                            out=acc[:, h : h + PASS],
+                            lhsT=emb_codes[:, i, :].bitcast(FP8X4),
+                            lhsT_scale=emb_scales[:, i, :],
+                            rhs=words[:, c + h : c + h + PASS].bitcast(FP8X4),
+                            rhs_scale=planes[4 * k : P, s : s + PASS],
+                            start=True,
+                            stop=True,
+                        )
+                    j = first_col + start + c
+                    nc.vector.tensor_tensor(
+                        out=residual[:, j : j + BANK],
+                        in0=grad[:, c : c + BANK],
+                        in1=acc[:],
+                        op=ALU.subtract,
+                    )
+                    squares = square_pool.tile([P, BANK], F32)
+                    nc.scalar.activation(
+                        out=squares[:],
+                        in_=residual[:, j : j + BANK],
+                        func=ACT.Square,
+                        accum_out=square_sums[:, j // BANK : j // BANK + 1],
+                    )
+                    if j // BANK < GPSIMD_BANKS:
+                        take_low(nc.gpsimd, j)
+            first_col += WIDTHS[i]
+
+        norm2 = keep.tile([P, 1], F32)
+        nc.vector.tensor_reduce(out=norm2[:], in_=square_sums[:], axis=AXIS.X, op=ALU.add)
+        nc.vector.tensor_scalar_max(out=norm2[:], in0=norm2[:], scalar1=1.0)
+        norm = keep.tile([P, 1], F32)
+        nc.scalar.sqrt(out=norm[:], in_=norm2[:])
+        factor = keep.tile([P, 1], F32)
+        nc.vector.reciprocal(out=factor[:], in_=norm[:])
+        factor_pair = keep.tile([P, 2], BF16)
+        nc.vector.tensor_copy(out=factor_pair[:, 0:1], in_=factor[:])
+        nc.vector.tensor_tensor(
+            out=factor_pair[:, 1:2], in0=factor[:], in1=factor_pair[:, 0:1], op=ALU.subtract
+        )
+        for bank in range(GPSIMD_BANKS, BANKS):
+            take_low(nc.vector, bank * BANK)
+
+        mean_ps = mean_pool.tile([P, BLOCKS, 2], F32)
+        for m in range(BLOCKS):
+            nc.tensor.matmul(
+                out=mean_ps[:, m, :], lhsT=high(m * P, P), rhs=factor_pair[:], start=True, stop=False
+            )
+            nc.tensor.matmul(
+                out=mean_ps[:, m, :],
+                lhsT=low[:, m * P : (m + 1) * P],
+                rhs=factor_pair[:],
+                start=False,
+                stop=True,
+            )
+        nc.vector.tensor_reduce(out=mean_sb[:, :BLOCKS], in_=mean_ps[:], axis=AXIS.X, op=ALU.add)
+
+        out_rows = out.rearrange("(m p) -> m p", p=P)
+        for half in range(2):
+            rows = min(P, BLOCKS - half * P)
+            flipped = flip_pool.tile([P, P], F32, tag="flip")
+            nc.tensor.transpose(flipped[:], mean_sb[:, half * P : (half + 1) * P], ident[:])
+            result = keep.tile([P, P], F32, name="result%d" % half)
+            nc.vector.tensor_scalar_mul(out=result[:], in0=flipped[:], scalar1=1.0 / P)
+            nc.sync.dma_start(out=out_rows[half * P : half * P + rows, :], in_=result[:rows, :])

@@ -182,6 +182,11 @@ def tile_gep_pb_kernel(
         for bank in range(GPSIMD_BANKS, BANKS):
             take_low(nc.vector, bank * BANK)
 
+        spare_ps = mean_pool.tile([P, BLOCKS, 2], F32)
+        for m in range(BLOCKS):
+            nc.tensor.matmul(
+                out=spare_ps[:, m, :], lhsT=high(m * P, P), rhs=factor_pair[:], start=True, stop=True
+            )
         mean_ps = mean_pool.tile([P, BLOCKS, 2], F32)
         for m in range(BLOCKS):
             nc.tensor.matmul(

@@ -182,21 +182,16 @@ def tile_gep_pb_kernel(
         for bank in range(GPSIMD_BANKS, BANKS):
             take_low(nc.vector, bank * BANK)
 
-        spare_ps = mean_pool.tile([P, BLOCKS, 2], F32)
+        mean_ps = mean_pool.tile([P, BLOCKS, 3], F32)
         for m in range(BLOCKS):
             nc.tensor.matmul(
-                out=spare_ps[:, m, :], lhsT=high(m * P, P), rhs=factor_pair[:], start=True, stop=True
-            )
-        mean_ps = mean_pool.tile([P, BLOCKS, 2], F32)
-        for m in range(BLOCKS):
-            nc.tensor.matmul(
-                out=mean_ps[:, m, :], lhsT=high(m * P, P), rhs=factor_pair[:], start=True, stop=False
+                out=mean_ps[:, m, 0:2], lhsT=high(m * P, P), rhs=factor_pair[:], start=True, stop=True
             )
             nc.tensor.matmul(
-                out=mean_ps[:, m, :],
+                out=mean_ps[:, m, 2:3],
                 lhsT=low[:, m * P : (m + 1) * P],
-                rhs=factor_pair[:],
-                start=False,
+                rhs=factor_pair[:, 0:1],
+                start=True,
                 stop=True,
             )
         nc.vector.tensor_reduce(out=mean_sb[:, :BLOCKS], in_=mean_ps[:], axis=AXIS.X, op=ALU.add)

@@ -75,9 +75,9 @@ def tile_gep_pb_kernel(
         for i in range(groups):
             cols = slice(plane_start[i], plane_start[i] + plane_cols[i])
             for quad in range(4):
-                rows = scales_in[i][0, 4 * quad : 4 * quad + 4, :].bitcast(I32)
-                nc.sync.dma_start(
-                    out=planes[32 * quad : 32 * quad + 4 * PLANES, cols].bitcast(I32),
+                rows = scales_in[i][0, 4 * quad : 4 * quad + 4, :].bitcast(F32)
+                nc.gpsimd.dma_start(
+                    out=planes[32 * quad : 32 * quad + 4 * PLANES, cols].bitcast(F32),
                     in_=rows.rearrange("r (k c) -> k r c", k=PLANES),
                 )
 

@@ -53,6 +53,7 @@ def tile_gep_pb_kernel(
         acc_pool = ctx.enter_context(tc.psum_pool(name="acc", bufs=4))
         flip_pool = ctx.enter_context(tc.psum_pool(name="flip", bufs=2))
         mean_pool = ctx.enter_context(tc.psum_pool(name="mean", bufs=1))
+        ctx.enter_context(tc.manual_schedule())
 
         plane_cols = [width // PLANES for width in WIDTHS]
         plane_start = [sum(plane_cols[:i]) for i in range(groups)]
@@ -75,9 +76,9 @@ def tile_gep_pb_kernel(
         for i in range(groups):
             cols = slice(plane_start[i], plane_start[i] + plane_cols[i])
             for quad in range(4):
-                rows = scales_in[i][0, 4 * quad : 4 * quad + 4, :].bitcast(F32)
-                nc.gpsimd.dma_start(
-                    out=planes[32 * quad : 32 * quad + 4 * PLANES, cols].bitcast(F32),
+                rows = scales_in[i][0, 4 * quad : 4 * quad + 4, :].bitcast(I32)
+                nc.sync.dma_start(
+                    out=planes[32 * quad : 32 * quad + 4 * PLANES, cols].bitcast(I32),
                     in_=rows.rearrange("r (k c) -> k r c", k=PLANES),
                 )
 

@@ -18,12 +18,12 @@ K_GROUP = 512
 WIDTHS = (4096, 9216, 7168)
 COLS = sum(WIDTHS)
 BANK = 512
+BANKS = COLS // BANK
 PASS = 256
 PLANES = 4
-PIECE = 3072
+PIECES = (3072, 3072, 1024)
 BLOCKS = COLS // P
-BANKS = COLS // BANK
-GPSIMD_BANKS = 26
+GPSIMD_BANKS = 18
 
 FLOPS = 2 * P * K_GROUP * COLS
 
@@ -113,24 +113,24 @@ def tile_gep_pb_kernel(
         def high(first, count):
             return halves[:, 2 * first + 1 : 2 * (first + count) : 2]
 
-        def take_low(engine, j):
+        def take_low(engine, first, count):
             engine.tensor_tensor(
-                out=low[:, j : j + BANK],
-                in0=residual[:, j : j + BANK],
-                in1=high(j, BANK),
+                out=low[:, first : first + count],
+                in0=residual[:, first : first + count],
+                in1=high(first, count),
                 op=ALU.subtract,
             )
 
         first_col = 0
         for i in range(groups):
             base_words = words_in[i].rearrange("o p n t -> (o p) (n t)").bitcast(I32)
-            for start in range(0, WIDTHS[i], PIECE):
-                width = min(PIECE, WIDTHS[i] - start)
-                words = words_pool.tile([P, PIECE], U32, align_bytes=64)
+            for start in range(0, WIDTHS[i], PIECES[i]):
+                width = min(PIECES[i], WIDTHS[i] - start)
+                words = words_pool.tile([P, max(PIECES)], U32, align_bytes=64)
                 nc.sync.dma_start(
                     out=words[:, :width].bitcast(I32), in_=base_words[:, start : start + width]
                 )
-                grad = grad_pool.tile([P, PIECE], BF16)
+                grad = grad_pool.tile([P, max(PIECES)], BF16)
                 nc.sync.dma_start(
                     out=grad[:, :width],
                     in_=target_grad[:, first_col + start : first_col + start + width],
@@ -165,7 +165,7 @@ def tile_gep_pb_kernel(
                         accum_out=square_sums[:, j // BANK : j // BANK + 1],
                     )
                     if j // BANK < GPSIMD_BANKS:
-                        take_low(nc.gpsimd, j)
+                        take_low(nc.gpsimd, j, BANK)
             first_col += WIDTHS[i]
 
         norm2 = keep.tile([P, 1], F32)
@@ -180,8 +180,8 @@ def tile_gep_pb_kernel(
         nc.vector.tensor_tensor(
             out=factor_pair[:, 1:2], in0=factor[:], in1=factor_pair[:, 0:1], op=ALU.subtract
         )
-        for bank in range(GPSIMD_BANKS, BANKS):
-            take_low(nc.vector, bank * BANK)
+        for bank in range(GPSIMD_BANKS, BANKS, 2):
+            take_low(nc.vector, bank * BANK, 2 * BANK)
 
         mean_ps = mean_pool.tile([P, BLOCKS, 3], F32)
         for m in range(BLOCKS):

@@ -76,9 +76,9 @@ def tile_gep_pb_kernel(
         for i in range(groups):
             cols = slice(plane_start[i], plane_start[i] + plane_cols[i])
             for quad in range(4):
-                rows = scales_in[i][0, 4 * quad : 4 * quad + 4, :].bitcast(I32)
-                nc.sync.dma_start(
-                    out=planes[32 * quad : 32 * quad + 4 * PLANES, cols].bitcast(I32),
+                rows = scales_in[i][0, 4 * quad : 4 * quad + 4, :].bitcast(F32)
+                nc.gpsimd.dma_start(
+                    out=planes[32 * quad : 32 * quad + 4 * PLANES, cols].bitcast(F32),
                     in_=rows.rearrange("r (k c) -> k r c", k=PLANES),
                 )
 

@@ -24,6 +24,7 @@ PLANES = 4
 PIECES = (3072, 3072, 1024)
 BLOCKS = COLS // P
 GPSIMD_BANKS = 18
+MEAN_N = 24
 
 FLOPS = 2 * P * K_GROUP * COLS
 
@@ -62,6 +63,9 @@ def tile_gep_pb_kernel(
 
         mean_sb = keep.tile([P, 2 * P], F32)
         nc.vector.memset(mean_sb[:], 0.0)
+
+        factor_pair = keep.tile([P, MEAN_N], BF16)
+        nc.vector.memset(factor_pair[:], 0.0)
 
         ident = keep.tile([P, P], F32)
         make_identity(nc, ident[:])
@@ -175,7 +179,6 @@ def tile_gep_pb_kernel(
         nc.scalar.sqrt(out=norm[:], in_=norm2[:])
         factor = keep.tile([P, 1], F32)
         nc.vector.reciprocal(out=factor[:], in_=norm[:])
-        factor_pair = keep.tile([P, 2], BF16)
         nc.vector.tensor_copy(out=factor_pair[:, 0:1], in_=factor[:])
         nc.vector.tensor_tensor(
             out=factor_pair[:, 1:2], in0=factor[:], in1=factor_pair[:, 0:1], op=ALU.subtract
@@ -183,19 +186,24 @@ def tile_gep_pb_kernel(
         for bank in range(GPSIMD_BANKS, BANKS, 2):
             take_low(nc.vector, bank * BANK, 2 * BANK)
 
-        mean_ps = mean_pool.tile([P, BLOCKS, 3], F32)
+        mean_ps = mean_pool.tile([P, BANK], F32)
         for m in range(BLOCKS):
             nc.tensor.matmul(
-                out=mean_ps[:, m, 0:2], lhsT=high(m * P, P), rhs=factor_pair[:], start=True, stop=True
+                out=mean_ps[:, 2 * m : 2 * m + MEAN_N], lhsT=high(m * P, P), rhs=factor_pair[:], start=True, stop=False
             )
             nc.tensor.matmul(
-                out=mean_ps[:, m, 2:3],
+                out=mean_ps[:, 2 * m : 2 * m + MEAN_N],
                 lhsT=low[:, m * P : (m + 1) * P],
-                rhs=factor_pair[:, 0:1],
-                start=True,
+                rhs=factor_pair[:],
+                start=False,
                 stop=True,
             )
-        nc.vector.tensor_reduce(out=mean_sb[:, :BLOCKS], in_=mean_ps[:], axis=AXIS.X, op=ALU.add)
+        nc.vector.tensor_reduce(
+            out=mean_sb[:, :BLOCKS],
+            in_=mean_ps[:, : 2 * BLOCKS].rearrange("p (m t) -> p m t", t=2),
+            axis=AXIS.X,
+            op=ALU.add,
+        )
 
         out_rows = out.rearrange("(m p) -> m p", p=P)
         for half in range(2):

@@ -23,7 +23,10 @@ PASS = 256
 PLANES = 4
 PIECES = (3072, 3072, 1024)
 BLOCKS = COLS // P
-GPSIMD_BANKS = 18
+ROUND = 5
+GPSIMD_SHARE = 3
+ROUNDS = BANKS // ROUND
+BANK_BLOCKS = BANK // P
 MEAN_N = 24
 
 FLOPS = 2 * P * K_GROUP * COLS
@@ -168,8 +171,8 @@ def tile_gep_pb_kernel(
                         func=ACT.Square,
                         accum_out=square_sums[:, j // BANK : j // BANK + 1],
                     )
-                    if j // BANK < GPSIMD_BANKS:
-                        take_low(nc.gpsimd, j, BANK)
+                    if (j // BANK) % ROUND == GPSIMD_SHARE - 1:
+                        take_low(nc.gpsimd, j - (GPSIMD_SHARE - 1) * BANK, GPSIMD_SHARE * BANK)
             first_col += WIDTHS[i]
 
         norm2 = keep.tile([P, 1], F32)
@@ -183,27 +186,37 @@ def tile_gep_pb_kernel(
         nc.vector.tensor_tensor(
             out=factor_pair[:, 1:2], in0=factor[:], in1=factor_pair[:, 0:1], op=ALU.subtract
         )
-        for bank in range(GPSIMD_BANKS, BANKS, 2):
-            take_low(nc.vector, bank * BANK, 2 * BANK)
+        for t in range(ROUNDS):
+            take_low(nc.vector, (t * ROUND + GPSIMD_SHARE) * BANK, (ROUND - GPSIMD_SHARE) * BANK)
 
-        mean_ps = mean_pool.tile([P, BANK], F32)
-        for m in range(BLOCKS):
-            nc.tensor.matmul(
-                out=mean_ps[:, 2 * m : 2 * m + MEAN_N], lhsT=high(m * P, P), rhs=factor_pair[:], start=True, stop=False
+        by_round = mean_sb[:, :BLOCKS].rearrange("p (t w) -> p t w", w=ROUND * BANK_BLOCKS)
+        for first, share in ((0, GPSIMD_SHARE), (GPSIMD_SHARE, ROUND - GPSIMD_SHARE)):
+            mean_ps = mean_pool.tile([P, BANK], F32, name="mean_ps%d" % first)
+            q = 0
+            for t in range(ROUNDS):
+                for w in range(share * BANK_BLOCKS):
+                    m = (t * ROUND + first) * BANK_BLOCKS + w
+                    nc.tensor.matmul(
+                        out=mean_ps[:, 2 * q : 2 * q + MEAN_N],
+                        lhsT=high(m * P, P),
+                        rhs=factor_pair[:],
+                        start=True,
+                        stop=False,
+                    )
+                    nc.tensor.matmul(
+                        out=mean_ps[:, 2 * q : 2 * q + MEAN_N],
+                        lhsT=low[:, m * P : (m + 1) * P],
+                        rhs=factor_pair[:],
+                        start=False,
+                        stop=True,
+                    )
+                    q += 1
+            nc.vector.tensor_reduce(
+                out=by_round[:, :, first * BANK_BLOCKS : (first + share) * BANK_BLOCKS],
+                in_=mean_ps[:, : 2 * q].rearrange("p (t w c) -> p t w c", t=ROUNDS, c=2),
+                axis=AXIS.X,
+                op=ALU.add,
             )
-            nc.tensor.matmul(
-                out=mean_ps[:, 2 * m : 2 * m + MEAN_N],
-                lhsT=low[:, m * P : (m + 1) * P],
-                rhs=factor_pair[:],
-                start=False,
-                stop=True,
-            )
-        nc.vector.tensor_reduce(
-            out=mean_sb[:, :BLOCKS],
-            in_=mean_ps[:, : 2 * BLOCKS].rearrange("p (m t) -> p m t", t=2),
-            axis=AXIS.X,
-            op=ALU.add,
-        )
 
         out_rows = out.rearrange("(m p) -> m p", p=P)
         for half in range(2):

@@ -24,8 +24,8 @@ PLANES = 4
 PIECES = (3072, 3072, 1024)
 BLOCKS = COLS // P
 ROUND = 5
-GPSIMD_SHARE = 3
-ROUNDS = BANKS // ROUND
+GPSIMD_SHARE = 4
+GPSIMD_ROUNDS = 6
 BANK_BLOCKS = BANK // P
 MEAN_N = 24
 
@@ -67,8 +67,10 @@ def tile_gep_pb_kernel(
         mean_sb = keep.tile([P, 2 * P], F32)
         nc.vector.memset(mean_sb[:], 0.0)
 
-        factor_pair = keep.tile([P, MEAN_N], BF16)
-        nc.vector.memset(factor_pair[:], 0.0)
+        factor_words = keep.tile([P, MEAN_N], F32)
+        nc.vector.memset(factor_words[:], 0.0)
+        factor_halves = factor_words[:].bitcast(BF16)
+        factor_pair = factor_halves[:, 1 : 2 * MEAN_N : 2]
 
         ident = keep.tile([P, P], F32)
         make_identity(nc, ident[:])
@@ -76,7 +78,7 @@ def tile_gep_pb_kernel(
         one = keep.tile([P, 1], F32)
         nc.vector.memset(one[:], 1.0)
         warm = keep.tile([P, 1], F32)
-        nc.scalar.sqrt(out=warm[:], in_=one[:])
+        nc.scalar.activation(out=warm[:], in_=one[:], func=ACT.Abs_reciprocal_sqrt)
 
         emb = keep.tile([P, groups * K_GROUP], BF16)
         nc.sync.dma_start(out=emb[:], in_=embedding)
@@ -171,52 +173,54 @@ def tile_gep_pb_kernel(
                         func=ACT.Square,
                         accum_out=square_sums[:, j // BANK : j // BANK + 1],
                     )
-                    if (j // BANK) % ROUND == GPSIMD_SHARE - 1:
+                    if (j // BANK) % ROUND == GPSIMD_SHARE - 1 and j // BANK < ROUND * GPSIMD_ROUNDS:
                         take_low(nc.gpsimd, j - (GPSIMD_SHARE - 1) * BANK, GPSIMD_SHARE * BANK)
             first_col += WIDTHS[i]
 
-        norm2 = keep.tile([P, 1], F32)
-        nc.vector.tensor_reduce(out=norm2[:], in_=square_sums[:], axis=AXIS.X, op=ALU.add)
-        nc.vector.tensor_scalar_max(out=norm2[:], in0=norm2[:], scalar1=1.0)
-        norm = keep.tile([P, 1], F32)
-        nc.scalar.sqrt(out=norm[:], in_=norm2[:])
-        factor = keep.tile([P, 1], F32)
-        nc.vector.reciprocal(out=factor[:], in_=norm[:])
-        nc.vector.tensor_copy(out=factor_pair[:, 0:1], in_=factor[:])
-        nc.vector.tensor_tensor(
-            out=factor_pair[:, 1:2], in0=factor[:], in1=factor_pair[:, 0:1], op=ALU.subtract
-        )
-        for t in range(ROUNDS):
-            take_low(nc.vector, (t * ROUND + GPSIMD_SHARE) * BANK, (ROUND - GPSIMD_SHARE) * BANK)
+        vector_stretches = [((t * ROUND + GPSIMD_SHARE) * BANK, (ROUND - GPSIMD_SHARE) * BANK) for t in range(GPSIMD_ROUNDS)]
+        vector_stretches += [(bank * BANK, 2 * BANK) for bank in range(ROUND * GPSIMD_ROUNDS, BANKS, 2)]
+        for first, count in vector_stretches:
+            take_low(nc.vector, first, count)
 
-        by_round = mean_sb[:, :BLOCKS].rearrange("p (t w) -> p t w", w=ROUND * BANK_BLOCKS)
-        for first, share in ((0, GPSIMD_SHARE), (GPSIMD_SHARE, ROUND - GPSIMD_SHARE)):
-            mean_ps = mean_pool.tile([P, BANK], F32, name="mean_ps%d" % first)
+        summed = keep.tile([P, BANKS], F32)
+        norm2 = keep.tile([P, 1], F32)
+        nc.scalar.activation(out=summed[:], in_=square_sums[:], func=ACT.Identity, accum_out=norm2[:])
+        excess = keep.tile([P, 1], F32)
+        nc.scalar.activation(out=excess[:], in_=norm2[:], func=ACT.Relu, bias=-1.0)
+        nc.scalar.activation(out=factor_words[:, 0:1], in_=excess[:], func=ACT.Abs_reciprocal_sqrt, bias=1.0)
+        nc.scalar.activation(
+            out=factor_halves[:, 3:4], in_=factor_halves[:, 1:2], func=ACT.Identity, scale=-1.0, bias=factor_words[:, 0:1]
+        )
+
+        def mean_of(stretches, name):
+            mean_ps = mean_pool.tile([P, BANK], F32, name=name)
             q = 0
-            for t in range(ROUNDS):
-                for w in range(share * BANK_BLOCKS):
-                    m = (t * ROUND + first) * BANK_BLOCKS + w
-                    nc.tensor.matmul(
-                        out=mean_ps[:, 2 * q : 2 * q + MEAN_N],
-                        lhsT=high(m * P, P),
-                        rhs=factor_pair[:],
-                        start=True,
-                        stop=False,
-                    )
-                    nc.tensor.matmul(
-                        out=mean_ps[:, 2 * q : 2 * q + MEAN_N],
-                        lhsT=low[:, m * P : (m + 1) * P],
-                        rhs=factor_pair[:],
-                        start=False,
-                        stop=True,
-                    )
+            for first, count in stretches:
+                for m in range(first // P, (first + count) // P):
+                    group = mean_ps[:, 2 * q : 2 * q + MEAN_N]
+                    nc.tensor.matmul(out=group, lhsT=high(m * P, P), rhs=factor_pair, start=True, stop=False)
+                    nc.tensor.matmul(out=group, lhsT=low[:, m * P : (m + 1) * P], rhs=factor_pair, start=False, stop=True)
                     q += 1
+            return mean_ps
+
+        def add_pairs(out, mean_ps, first, count, rounds):
             nc.vector.tensor_reduce(
-                out=by_round[:, :, first * BANK_BLOCKS : (first + share) * BANK_BLOCKS],
-                in_=mean_ps[:, : 2 * q].rearrange("p (t w c) -> p t w c", t=ROUNDS, c=2),
+                out=out,
+                in_=mean_ps[:, 2 * first : 2 * (first + count)].rearrange("p (t w c) -> p t w c", t=rounds, c=2),
                 axis=AXIS.X,
                 op=ALU.add,
             )
+
+        round_blocks = ROUND * BANK_BLOCKS
+        share_blocks = GPSIMD_SHARE * BANK_BLOCKS
+        shared = GPSIMD_ROUNDS * round_blocks
+        by_round = mean_sb[:, :shared].rearrange("p (t w) -> p t w", w=round_blocks)
+        gpsimd_ps = mean_of([(t * ROUND * BANK, GPSIMD_SHARE * BANK) for t in range(GPSIMD_ROUNDS)], "gpsimd_ps")
+        add_pairs(by_round[:, :, :share_blocks], gpsimd_ps, 0, GPSIMD_ROUNDS * share_blocks, GPSIMD_ROUNDS)
+        vector_ps = mean_of(vector_stretches, "vector_ps")
+        rest = GPSIMD_ROUNDS * (round_blocks - share_blocks)
+        add_pairs(by_round[:, :, share_blocks:], vector_ps, 0, rest, GPSIMD_ROUNDS)
+        add_pairs(mean_sb[:, shared:BLOCKS].unsqueeze(1), vector_ps, rest, BLOCKS - shared, 1)
 
         out_rows = out.rearrange("(m p) -> m p", p=P)
         for half in range(2):

@@ -29,6 +29,8 @@ GPSIMD_ROUNDS = 6
 BANK_BLOCKS = BANK // P
 MEAN_N = 24
 
+IDLE_PASSES = 16
+
 FLOPS = 2 * P * K_GROUP * COLS
 
 
@@ -176,6 +178,18 @@ def tile_gep_pb_kernel(
                     if (j // BANK) % ROUND == GPSIMD_SHARE - 1 and j // BANK < ROUND * GPSIMD_ROUNDS:
                         take_low(nc.gpsimd, j - (GPSIMD_SHARE - 1) * BANK, GPSIMD_SHARE * BANK)
             first_col += WIDTHS[i]
+
+        idle = acc_pool.tile([P, BANK], F32, name="acc")
+        for r in range(IDLE_PASSES):
+            nc.tensor.matmul_mx(
+                out=idle[:, :PASS],
+                lhsT=emb_codes[:, i, :].bitcast(FP8X4),
+                lhsT_scale=emb_scales[:, i, :],
+                rhs=words[:, c + h : c + h + PASS].bitcast(FP8X4),
+                rhs_scale=planes[4 * k : P, s : s + PASS],
+                start=True,
+                stop=True,
+            )
 
         vector_stretches = [((t * ROUND + GPSIMD_SHARE) * BANK, (ROUND - GPSIMD_SHARE) * BANK) for t in range(GPSIMD_ROUNDS)]
         vector_stretches += [(bank * BANK, 2 * BANK) for bank in range(ROUND * GPSIMD_ROUNDS, BANKS, 2)]

@@ -21,7 +21,13 @@ BANK = 512
 BANKS = COLS // BANK
 PASS = 256
 PLANES = 4
-PIECES = (3072, 3072, 1024)
+PIECES = (
+    (2048, 2048),
+    (2048, 2048, 2048, 2048, 1024),
+    (2048, 2048, 1024, 1024, 512, 512),
+)
+PIECE_MAX = 2048
+PIECE_BUFS = 7
 BLOCKS = COLS // P
 ROUND = 5
 GPSIMD_SHARE = 4
@@ -53,8 +59,8 @@ def tile_gep_pb_kernel(
 
     with ExitStack() as ctx:
         keep = ctx.enter_context(tc.tile_pool(name="keep", bufs=1))
-        words_pool = ctx.enter_context(tc.tile_pool(name="words", bufs=4))
-        grad_pool = ctx.enter_context(tc.tile_pool(name="grad", bufs=4))
+        words_pool = ctx.enter_context(tc.tile_pool(name="words", bufs=PIECE_BUFS))
+        grad_pool = ctx.enter_context(tc.tile_pool(name="grad", bufs=PIECE_BUFS))
         square_pool = ctx.enter_context(tc.tile_pool(name="square", bufs=3))
         acc_pool = ctx.enter_context(tc.psum_pool(name="acc", bufs=4))
         flip_pool = ctx.enter_context(tc.psum_pool(name="flip", bufs=2))
@@ -135,13 +141,14 @@ def tile_gep_pb_kernel(
         first_col = 0
         for i in range(groups):
             base_words = words_in[i].rearrange("o p n t -> (o p) (n t)").bitcast(I32)
-            for start in range(0, WIDTHS[i], PIECES[i]):
-                width = min(PIECES[i], WIDTHS[i] - start)
-                words = words_pool.tile([P, max(PIECES)], U32, align_bytes=64)
+            assert sum(PIECES[i]) == WIDTHS[i]
+            for piece, width in enumerate(PIECES[i]):
+                start = sum(PIECES[i][:piece])
+                words = words_pool.tile([P, PIECE_MAX], U32, align_bytes=64)
                 nc.sync.dma_start(
                     out=words[:, :width].bitcast(I32), in_=base_words[:, start : start + width]
                 )
-                grad = grad_pool.tile([P, max(PIECES)], BF16)
+                grad = grad_pool.tile([P, PIECE_MAX], BF16)
                 nc.sync.dma_start(
                     out=grad[:, :width],
                     in_=target_grad[:, first_col + start : first_col + start + width],

@@ -28,11 +28,12 @@ PIECES = (
 )
 PIECE_MAX = 2048
 PIECE_BUFS = 7
+GPSIMD_BANKS = 24
+GPSIMD_STEP = 4
+VECTOR_STEP = 2
+GPSIMD_COLS = GPSIMD_BANKS * BANK
+VECTOR_COLS = COLS - GPSIMD_COLS
 BLOCKS = COLS // P
-ROUND = 5
-GPSIMD_SHARE = 4
-GPSIMD_ROUNDS = 6
-BANK_BLOCKS = BANK // P
 MEAN_N = 24
 
 IDLE_PASSES = 16
@@ -182,8 +183,8 @@ def tile_gep_pb_kernel(
                         func=ACT.Square,
                         accum_out=square_sums[:, j // BANK : j // BANK + 1],
                     )
-                    if (j // BANK) % ROUND == GPSIMD_SHARE - 1 and j // BANK < ROUND * GPSIMD_ROUNDS:
-                        take_low(nc.gpsimd, j - (GPSIMD_SHARE - 1) * BANK, GPSIMD_SHARE * BANK)
+                    if j + BANK <= GPSIMD_COLS and (j + BANK) % (GPSIMD_STEP * BANK) == 0:
+                        take_low(nc.gpsimd, j + BANK - GPSIMD_STEP * BANK, GPSIMD_STEP * BANK)
             first_col += WIDTHS[i]
 
         idle = acc_pool.tile([P, BANK], F32, name="acc")
@@ -198,56 +199,55 @@ def tile_gep_pb_kernel(
                 stop=True,
             )
 
-        vector_stretches = [((t * ROUND + GPSIMD_SHARE) * BANK, (ROUND - GPSIMD_SHARE) * BANK) for t in range(GPSIMD_ROUNDS)]
-        vector_stretches += [(bank * BANK, 2 * BANK) for bank in range(ROUND * GPSIMD_ROUNDS, BANKS, 2)]
-        for first, count in vector_stretches:
-            take_low(nc.vector, first, count)
-
         summed = keep.tile([P, BANKS], F32)
         norm2 = keep.tile([P, 1], F32)
         nc.scalar.activation(out=summed[:], in_=square_sums[:], func=ACT.Identity, accum_out=norm2[:])
         excess = keep.tile([P, 1], F32)
         nc.scalar.activation(out=excess[:], in_=norm2[:], func=ACT.Relu, bias=-1.0)
-        nc.scalar.activation(out=factor_words[:, 0:1], in_=excess[:], func=ACT.Abs_reciprocal_sqrt, bias=1.0)
+        nc.scalar.activation(
+            out=factor_words[:, 0:1], in_=excess[:], func=ACT.Abs_reciprocal_sqrt, scale=float(P * P), bias=float(P * P)
+        )
         nc.scalar.activation(
             out=factor_halves[:, 3:4], in_=factor_halves[:, 1:2], func=ACT.Identity, scale=-1.0, bias=factor_words[:, 0:1]
         )
 
-        def mean_of(stretches, name):
-            mean_ps = mean_pool.tile([P, BANK], F32, name=name)
-            q = 0
-            for first, count in stretches:
-                for m in range(first // P, (first + count) // P):
-                    group = mean_ps[:, 2 * q : 2 * q + MEAN_N]
-                    nc.tensor.matmul(out=group, lhsT=high(m * P, P), rhs=factor_pair, start=True, stop=False)
-                    nc.tensor.matmul(out=group, lhsT=low[:, m * P : (m + 1) * P], rhs=factor_pair, start=False, stop=True)
-                    q += 1
-            return mean_ps
+        for first in range(GPSIMD_COLS, COLS, VECTOR_STEP * BANK):
+            take_low(nc.vector, first, VECTOR_STEP * BANK)
 
-        def add_pairs(out, mean_ps, first, count, rounds):
+        out_rows = out.rearrange("(m p) -> m p", p=P)
+
+        def block_means(mean_ps, first, last):
+            for m in range(first, last):
+                group = mean_ps[:, 2 * (m % P) : 2 * (m % P) + MEAN_N]
+                nc.tensor.matmul(out=group, lhsT=high(m * P, P), rhs=factor_pair, start=True, stop=False)
+                nc.tensor.matmul(out=group, lhsT=low[:, m * P : (m + 1) * P], rhs=factor_pair, start=False, stop=True)
+
+        def add_pairs(mean_ps, first, last):
             nc.vector.tensor_reduce(
-                out=out,
-                in_=mean_ps[:, 2 * first : 2 * (first + count)].rearrange("p (t w c) -> p t w c", t=rounds, c=2),
+                out=mean_sb[:, first:last],
+                in_=mean_ps[:, : 2 * (last - first)].rearrange("p (m c) -> p m c", c=2),
                 axis=AXIS.X,
                 op=ALU.add,
             )
 
-        round_blocks = ROUND * BANK_BLOCKS
-        share_blocks = GPSIMD_SHARE * BANK_BLOCKS
-        shared = GPSIMD_ROUNDS * round_blocks
-        by_round = mean_sb[:, :shared].rearrange("p (t w) -> p t w", w=round_blocks)
-        gpsimd_ps = mean_of([(t * ROUND * BANK, GPSIMD_SHARE * BANK) for t in range(GPSIMD_ROUNDS)], "gpsimd_ps")
-        add_pairs(by_round[:, :, :share_blocks], gpsimd_ps, 0, GPSIMD_ROUNDS * share_blocks, GPSIMD_ROUNDS)
-        vector_ps = mean_of(vector_stretches, "vector_ps")
-        rest = GPSIMD_ROUNDS * (round_blocks - share_blocks)
-        add_pairs(by_round[:, :, share_blocks:], vector_ps, 0, rest, GPSIMD_ROUNDS)
-        add_pairs(mean_sb[:, shared:BLOCKS].unsqueeze(1), vector_ps, rest, BLOCKS - shared, 1)
-
-        out_rows = out.rearrange("(m p) -> m p", p=P)
-        for half in range(2):
-            rows = min(P, BLOCKS - half * P)
+        def flip(first):
             flipped = flip_pool.tile([P, P], F32, tag="flip")
-            nc.tensor.transpose(flipped[:], mean_sb[:, half * P : (half + 1) * P], ident[:])
-            result = keep.tile([P, P], F32, name="result%d" % half)
-            nc.vector.tensor_scalar_mul(out=result[:], in0=flipped[:], scalar1=1.0 / P)
-            nc.sync.dma_start(out=out_rows[half * P : half * P + rows, :], in_=result[:rows, :])
+            nc.tensor.transpose(flipped[:], mean_sb[:, first : first + P], ident[:])
+            return flipped
+
+        first_ps = mean_pool.tile([P, BANK], F32)
+        block_means(first_ps, 0, P)
+        add_pairs(first_ps, 0, P)
+        rest_ps = mean_pool.tile([P, BANK], F32)
+        middle = (P + BLOCKS) // 2
+        block_means(rest_ps, P, middle)
+        first_flipped = flip(0)
+        first_result = keep.tile([P, P], F32)
+        nc.scalar.copy(out=first_result[:], in_=first_flipped[:])
+        nc.scalar.dma_start(out=out_rows[:P, :], in_=first_result[:])
+        block_means(rest_ps, middle, BLOCKS)
+        add_pairs(rest_ps, P, BLOCKS)
+        rest_flipped = flip(P)
+        rest_result = keep.tile([P, P], F32)
+        nc.vector.tensor_copy(out=rest_result[:], in_=rest_flipped[:])
+        nc.sync.dma_start(out=out_rows[P:, :], in_=rest_result[: BLOCKS - P, :])

@@ -24,8 +24,9 @@ PLANES = 4
 PIECES = (
     (2048, 2048),
     (2048, 2048, 2048, 2048, 1024),
-    (2048, 2048, 1024, 1024, 512, 512),
+    (2048, 2048, 1024, 1024, 512, 256, 256),
 )
+CHUNKS = sum(-(-width // BANK) for widths in PIECES for width in widths)
 PIECE_MAX = 2048
 PIECE_BUFS = 7
 GPSIMD_BANKS = 24
@@ -124,7 +125,11 @@ def tile_gep_pb_kernel(
             )
 
         residual = keep.tile([P, COLS], F32)
-        square_sums = keep.tile([P, BANKS], F32)
+        square_sums = keep.tile([P, 1 + CHUNKS], F32)
+        nc.vector.memset(square_sums[:, 0:1], -1.0)
+        summed = keep.tile([P, CHUNKS], F32)
+        early_sum = keep.tile([P, 1], F32)
+        chunk = 0
         halves = residual[:].bitcast(BF16)
         low = keep.tile([P, COLS], BF16)
 
@@ -155,8 +160,9 @@ def tile_gep_pb_kernel(
                     in_=target_grad[:, first_col + start : first_col + start + width],
                 )
                 for c in range(0, width, BANK):
+                    cols = min(BANK, width - c)
                     acc = acc_pool.tile([P, BANK], F32)
-                    for h in range(0, BANK, PASS):
+                    for h in range(0, cols, PASS):
                         n = start + c + h
                         k = n // plane_cols[i]
                         s = plane_start[i] + n % plane_cols[i]
@@ -171,20 +177,25 @@ def tile_gep_pb_kernel(
                         )
                     j = first_col + start + c
                     nc.vector.tensor_tensor(
-                        out=residual[:, j : j + BANK],
-                        in0=grad[:, c : c + BANK],
-                        in1=acc[:],
+                        out=residual[:, j : j + cols],
+                        in0=grad[:, c : c + cols],
+                        in1=acc[:, :cols],
                         op=ALU.subtract,
                     )
+                    chunk += 1
+                    if chunk == CHUNKS:
+                        nc.scalar.activation(
+                            out=summed[:], in_=square_sums[:, :CHUNKS], func=ACT.Identity, accum_out=early_sum[:]
+                        )
                     squares = square_pool.tile([P, BANK], F32)
                     nc.scalar.activation(
-                        out=squares[:],
-                        in_=residual[:, j : j + BANK],
+                        out=squares[:, :cols],
+                        in_=residual[:, j : j + cols],
                         func=ACT.Square,
-                        accum_out=square_sums[:, j // BANK : j // BANK + 1],
+                        accum_out=square_sums[:, chunk : chunk + 1],
                     )
-                    if j + BANK <= GPSIMD_COLS and (j + BANK) % (GPSIMD_STEP * BANK) == 0:
-                        take_low(nc.gpsimd, j + BANK - GPSIMD_STEP * BANK, GPSIMD_STEP * BANK)
+                    if j + cols <= GPSIMD_COLS and (j + cols) % (GPSIMD_STEP * BANK) == 0:
+                        take_low(nc.gpsimd, j + cols - GPSIMD_STEP * BANK, GPSIMD_STEP * BANK)
             first_col += WIDTHS[i]
 
         idle = acc_pool.tile([P, BANK], F32, name="acc")
@@ -199,11 +210,8 @@ def tile_gep_pb_kernel(
                 stop=True,
             )
 
-        summed = keep.tile([P, BANKS], F32)
-        norm2 = keep.tile([P, 1], F32)
-        nc.scalar.activation(out=summed[:], in_=square_sums[:], func=ACT.Identity, accum_out=norm2[:])
         excess = keep.tile([P, 1], F32)
-        nc.scalar.activation(out=excess[:], in_=norm2[:], func=ACT.Relu, bias=-1.0)
+        nc.scalar.activation(out=excess[:], in_=square_sums[:, CHUNKS : CHUNKS + 1], func=ACT.Relu, bias=early_sum[:])
         nc.scalar.activation(
             out=factor_words[:, 0:1], in_=excess[:], func=ACT.Abs_reciprocal_sqrt, scale=float(P * P), bias=float(P * P)
         )

from contextlib import ExitStack

import concourse.mybir as mybir
from concourse.masks import make_identity

F32 = mybir.dt.float32
BF16 = mybir.dt.bfloat16
I32 = mybir.dt.int32
U32 = mybir.dt.uint32
U8 = mybir.dt.uint8
FP8X4 = mybir.dt.float8_e4m3fn_x4
ALU = mybir.AluOpType
ACT = mybir.ActivationFunctionType
AXIS = mybir.AxisListType

P = 128
K_GROUP = 512
WIDTHS = (4096, 9216, 7168)
COLS = sum(WIDTHS)
BANK = 512
BANKS = COLS // BANK
PASS = 256
PLANES = 4
PIECES = (
    (2048, 2048),
    (2048, 2048, 2048, 2048, 1024),
    (2048, 2048, 1024, 1024, 512, 256, 256),
)
CHUNKS = sum(-(-width // BANK) for widths in PIECES for width in widths)
PIECE_MAX = 2048
PIECE_BUFS = 7
GPSIMD_BANKS = 24
GPSIMD_STEP = 4
VECTOR_STEP = 2
GPSIMD_COLS = GPSIMD_BANKS * BANK
VECTOR_COLS = COLS - GPSIMD_COLS
BLOCKS = COLS // P
MEAN_N = 24

IDLE_PASSES = 16

FLOPS = 2 * P * K_GROUP * COLS


def tile_gep_pb_kernel(
    tc,
    target_grad,
    embedding,
    bases0_words,
    bases0_scales,
    bases1_words,
    bases1_scales,
    bases2_words,
    bases2_scales,
    out,
):
    nc = tc.nc
    words_in = (bases0_words, bases1_words, bases2_words)
    scales_in = (bases0_scales, bases1_scales, bases2_scales)
    groups = len(WIDTHS)

    with ExitStack() as ctx:
        keep = ctx.enter_context(tc.tile_pool(name="keep", bufs=1))
        words_pool = ctx.enter_context(tc.tile_pool(name="words", bufs=PIECE_BUFS))
        grad_pool = ctx.enter_context(tc.tile_pool(name="grad", bufs=PIECE_BUFS))
        square_pool = ctx.enter_context(tc.tile_pool(name="square", bufs=3))
        acc_pool = ctx.enter_context(tc.psum_pool(name="acc", bufs=4))
        flip_pool = ctx.enter_context(tc.psum_pool(name="flip", bufs=2))
        mean_pool = ctx.enter_context(tc.psum_pool(name="mean", bufs=1))
        ctx.enter_context(tc.manual_schedule())

        plane_cols = [width // PLANES for width in WIDTHS]
        plane_start = [sum(plane_cols[:i]) for i in range(groups)]
        planes = keep.tile([P, sum(plane_cols)], U8, align_bytes=64)
        nc.vector.memset(planes[:].bitcast(I32), 0)

        mean_sb = keep.tile([P, 2 * P], F32)
        nc.vector.memset(mean_sb[:], 0.0)

        factor_words = keep.tile([P, MEAN_N], F32)
        nc.vector.memset(factor_words[:], 0.0)
        factor_halves = factor_words[:].bitcast(BF16)
        factor_pair = factor_halves[:, 1 : 2 * MEAN_N : 2]

        ident = keep.tile([P, P], F32)
        make_identity(nc, ident[:])

        one = keep.tile([P, 1], F32)
        nc.vector.memset(one[:], 1.0)
        warm = keep.tile([P, 1], F32)
        nc.scalar.activation(out=warm[:], in_=one[:], func=ACT.Abs_reciprocal_sqrt)

        emb = keep.tile([P, groups * K_GROUP], BF16)
        nc.sync.dma_start(out=emb[:], in_=embedding)
        for i in range(groups):
            cols = slice(plane_start[i], plane_start[i] + plane_cols[i])
            for quad in range(4):
                rows = scales_in[i][0, 4 * quad : 4 * quad + 4, :].bitcast(F32)
                nc.gpsimd.dma_start(
                    out=planes[32 * quad : 32 * quad + 4 * PLANES, cols].bitcast(F32),
                    in_=rows.rearrange("r (k c) -> k r c", k=PLANES),
                )

        emb_words = emb[:].bitcast(F32)
        grouped = keep.tile([P, groups, 4 * P], BF16, align_bytes=64)
        emb_codes = keep.tile([P, groups, P], U32, align_bytes=64)
        emb_scales = keep.tile([P, groups, P], U8, align_bytes=64)
        for i in range(groups):
            flipped = flip_pool.tile([P, 2, P], F32, tag="flip")
            for u in range(2):
                nc.tensor.transpose(
                    flipped[:, u, :],
                    emb_words[:, 256 * i + u : 256 * (i + 1) : 2],
                    ident[:],
                )
            nc.vector.tensor_copy(
                out=grouped[:, i, :].bitcast(F32).rearrange("p (b u) -> p b u", u=2),
                in_=flipped[:].rearrange("p u b -> p b u"),
            )
        for i in range(groups):
            nc.vector.quantize_mx(
                out=emb_codes[:, i, :].bitcast(FP8X4),
                scales=emb_scales[:, i, :],
                in_=grouped[:, i, :],
            )

        residual = keep.tile([P, COLS], F32)
        square_sums = keep.tile([P, 1 + CHUNKS], F32)
        nc.vector.memset(square_sums[:, 0:1], -1.0)
        summed = keep.tile([P, CHUNKS], F32)
        early_sum = keep.tile([P, 1], F32)
        chunk = 0
        halves = residual[:].bitcast(BF16)
        low = keep.tile([P, COLS], BF16)

        def high(first, count):
            return halves[:, 2 * first + 1 : 2 * (first + count) : 2]

        def take_low(engine, first, count):
            engine.tensor_tensor(
                out=low[:, first : first + count],
                in0=residual[:, first : first + count],
                in1=high(first, count),
                op=ALU.subtract,
            )

        first_col = 0
        for i in range(groups):
            base_words = words_in[i].rearrange("o p n t -> (o p) (n t)").bitcast(I32)
            assert sum(PIECES[i]) == WIDTHS[i]
            for piece, width in enumerate(PIECES[i]):
                start = sum(PIECES[i][:piece])
                words = words_pool.tile([P, PIECE_MAX], U32, align_bytes=64)
                nc.sync.dma_start(
                    out=words[:, :width].bitcast(I32), in_=base_words[:, start : start + width]
                )
                grad = grad_pool.tile([P, PIECE_MAX], BF16)
                nc.sync.dma_start(
                    out=grad[:, :width],
                    in_=target_grad[:, first_col + start : first_col + start + width],
                )
                for c in range(0, width, BANK):
                    cols = min(BANK, width - c)
                    acc = acc_pool.tile([P, BANK], F32)
                    for h in range(0, cols, PASS):
                        n = start + c + h
                        k = n // plane_cols[i]
                        s = plane_start[i] + n % plane_cols[i]
                        nc.tensor.matmul_mx(
                            out=acc[:, h : h + PASS],
                            lhsT=emb_codes[:, i, :].bitcast(FP8X4),
                            lhsT_scale=emb_scales[:, i, :],
                            rhs=words[:, c + h : c + h + PASS].bitcast(FP8X4),
                            rhs_scale=planes[4 * k : P, s : s + PASS],
                            start=True,
                            stop=True,
                        )
                    j = first_col + start + c
                    nc.vector.tensor_tensor(
                        out=residual[:, j : j + cols],
                        in0=grad[:, c : c + cols],
                        in1=acc[:, :cols],
                        op=ALU.subtract,
                    )
                    chunk += 1
                    if chunk == CHUNKS:
                        nc.scalar.activation(
                            out=summed[:], in_=square_sums[:, :CHUNKS], func=ACT.Identity, accum_out=early_sum[:]
                        )
                    squares = square_pool.tile([P, BANK], F32)
                    nc.scalar.activation(
                        out=squares[:, :cols],
                        in_=residual[:, j : j + cols],
                        func=ACT.Square,
                        accum_out=square_sums[:, chunk : chunk + 1],
                    )
                    if j + cols <= GPSIMD_COLS and (j + cols) % (GPSIMD_STEP * BANK) == 0:
                        take_low(nc.gpsimd, j + cols - GPSIMD_STEP * BANK, GPSIMD_STEP * BANK)
            first_col += WIDTHS[i]

        idle = acc_pool.tile([P, BANK], F32, name="acc")
        for r in range(IDLE_PASSES):
            nc.tensor.matmul_mx(
                out=idle[:, :PASS],
                lhsT=emb_codes[:, i, :].bitcast(FP8X4),
                lhsT_scale=emb_scales[:, i, :],
                rhs=words[:, c + h : c + h + PASS].bitcast(FP8X4),
                rhs_scale=planes[4 * k : P, s : s + PASS],
                start=True,
                stop=True,
            )

        excess = keep.tile([P, 1], F32)
        nc.scalar.activation(out=excess[:], in_=square_sums[:, CHUNKS : CHUNKS + 1], func=ACT.Relu, bias=early_sum[:])
        nc.scalar.activation(
            out=factor_words[:, 0:1], in_=excess[:], func=ACT.Abs_reciprocal_sqrt, scale=float(P * P), bias=float(P * P)
        )
        nc.scalar.activation(
            out=factor_halves[:, 3:4], in_=factor_halves[:, 1:2], func=ACT.Identity, scale=-1.0, bias=factor_words[:, 0:1]
        )

        for first in range(GPSIMD_COLS, COLS, VECTOR_STEP * BANK):
            take_low(nc.vector, first, VECTOR_STEP * BANK)

        out_rows = out.rearrange("(m p) -> m p", p=P)

        def block_means(mean_ps, first, last):
            for m in range(first, last):
                group = mean_ps[:, 2 * (m % P) : 2 * (m % P) + MEAN_N]
                nc.tensor.matmul(out=group, lhsT=high(m * P, P), rhs=factor_pair, start=True, stop=False)
                nc.tensor.matmul(out=group, lhsT=low[:, m * P : (m + 1) * P], rhs=factor_pair, start=False, stop=True)

        def add_pairs(mean_ps, first, last):
            nc.vector.tensor_reduce(
                out=mean_sb[:, first:last],
                in_=mean_ps[:, : 2 * (last - first)].rearrange("p (m c) -> p m c", c=2),
                axis=AXIS.X,
                op=ALU.add,
            )

        def flip(first):
            flipped = flip_pool.tile([P, P], F32, tag="flip")
            nc.tensor.transpose(flipped[:], mean_sb[:, first : first + P], ident[:])
            return flipped

        first_ps = mean_pool.tile([P, BANK], F32)
        block_means(first_ps, 0, P)
        add_pairs(first_ps, 0, P)
        rest_ps = mean_pool.tile([P, BANK], F32)
        middle = (P + BLOCKS) // 2
        block_means(rest_ps, P, middle)
        first_flipped = flip(0)
        first_result = keep.tile([P, P], F32)
        nc.scalar.copy(out=first_result[:], in_=first_flipped[:])
        nc.scalar.dma_start(out=out_rows[:P, :], in_=first_result[:])
        block_means(rest_ps, middle, BLOCKS)
        add_pairs(rest_ps, P, BLOCKS)
        rest_flipped = flip(P)
        rest_result = keep.tile([P, P], F32)
        nc.vector.tensor_copy(out=rest_result[:], in_=rest_flipped[:])
        nc.sync.dma_start(out=out_rows[P:, :], in_=rest_result[: BLOCKS - P, :])
